import numpy as np
import ml_dtypes


def mxq(x, axis, fmt="e4m3"):
    dtype, down = {"e4m3": (ml_dtypes.float8_e4m3fn, 7), "e5m2": (ml_dtypes.float8_e5m2, 14)}[fmt]
    v = np.moveaxis(np.asarray(x, np.float32).astype(ml_dtypes.bfloat16).astype(np.float64), axis, -1)
    blocks = v.reshape(v.shape[:-1] + (-1, 32))
    amax = np.abs(blocks).max(-1, keepdims=True)
    byte = np.maximum(np.where(amax > 0, np.frexp(amax)[1] - 1 + 127, 0) - down, 1)
    scale = np.exp2(byte - 127.0)
    codes = (blocks / scale).astype(np.float32).astype(dtype).astype(np.float64)
    return np.moveaxis((codes * scale).reshape(v.shape), -1, axis)


WIDE = False


def mx_kscale(k):
    if not WIDE:
        return np.ones(k)
    levels = np.array([10, -10, 5, -5, 0])
    a = np.random.permutation(np.resize(levels, k // 512 * 4)).reshape(k // 512, 4)
    idx = np.arange(k)
    return np.exp2(a[idx // 512, idx % 128 // 32])


BF16 = ml_dtypes.bfloat16


def bf(x):
    return np.asarray(x, np.float32).astype(BF16)


def f64(x):
    return np.asarray(x).astype(np.float64)


E2M1 = np.array([0.0, 0.5, 1.0, 1.5, 2.0, 3.0, 4.0, 6.0, -0.0, -0.5, -1.0, -1.5, -2.0, -3.0, -4.0, -6.0])


def pack_weight(w, fmt):
    k, n = w.shape
    w = f64(bf(w)).reshape(k // 32, 32, n)
    amax = np.abs(w).max(1)
    if fmt == "e4m3":
        byte = np.frexp(amax)[1] - 1 + 127 - 7
    else:
        mant, ex = np.frexp(amax / 6.0)
        byte = np.where(mant > 0.5, ex, ex - 1) + 127
    byte = np.clip(np.where(amax > 0, byte, 1), 1, 254)
    scaled = (w * np.exp2(127.0 - byte)[:, None, :]).reshape(k, n).astype(np.float32)
    by_word = np.ascontiguousarray(scaled.reshape(k // 512, 128, 4, n).transpose(0, 1, 3, 2))
    if fmt == "e4m3":
        words = by_word.astype(ml_dtypes.float8_e4m3fn).view(np.uint8)
    else:
        c = by_word.astype(ml_dtypes.float4_e2m1fn).view(np.uint8) & 0xF
        words = c[..., 0::2] | (c[..., 1::2] << 4)
    return np.ascontiguousarray(words), np.ascontiguousarray(byte.astype(np.uint8).reshape(k // 512, 16, n))


def unpack_weight(words, scales, fmt):
    g, p, n, _ = words.shape
    if fmt == "e4m3":
        vals = np.ascontiguousarray(words).view(ml_dtypes.float8_e4m3fn).astype(np.float64)
    else:
        nib = np.empty((g, p, n, 4), np.uint8)
        nib[..., 0::2] = words & 0xF
        nib[..., 1::2] = words >> 4
        vals = E2M1[nib]
    vals = vals * np.repeat(np.exp2(scales.astype(np.float64) - 127.0), 8, axis=1)[..., None]
    return vals.transpose(0, 1, 3, 2).reshape(g * 512, n)


B, IN, OUT, R, Q, ORD = 1024, 1024, 1024, 4, 256, 7
K = R ** ORD


def setup_inputs():
    s = mx_kscale(K)[np.arange(R) * (K // R + R)]
    z = np.random.standard_normal((ORD, R, B))
    z[ORD - 1] *= s[:, None]
    g = np.random.standard_normal((Q, K)) / np.sqrt(K) / np.repeat(s, K // R)
    words, scales = pack_weight(np.ascontiguousarray(g.T), "e4m3")
    return {"z": bf(z), "G2_words": words, "G2_scales": scales}


def reference(z, G2_words, G2_scales):
    Z = f64(z)
    kron = Z[0]
    for j in range(1, ORD):
        kron = kron[None] * Z[j].reshape((R,) + (1,) * j + (B,))
    kron = kron.reshape((-1, B))
    return unpack_weight(G2_words, G2_scales, "e4m3").T @ mxq(kron, 0, "e4m3")

@@ -1,0 +1,211 @@
+from contextlib import ExitStack
+
+import concourse.mybir as mybir
+from concourse.masks import make_identity
+
+F32 = mybir.dt.float32
+BF16 = mybir.dt.bfloat16
+I32 = mybir.dt.int32
+U32 = mybir.dt.uint32
+U8 = mybir.dt.uint8
+FP8X4 = mybir.dt.float8_e4m3fn_x4
+MULT = mybir.AluOpType.mult
+COPY = mybir.ActivationFunctionType.Copy
+
+P = 128
+RANK = 4
+ORDER = 7
+SAMPLES = 1024
+ROWS = 256
+PASSES = 32
+SAMPLE_TILES = SAMPLES // P
+HALF = 512
+TILES_PER_HALF = HALF // P
+LOW = RANK**5
+STEPS = 2 * RANK * RANK
+SCALAR_EVERY = 5
+
+FLOPS = 2 * ROWS * RANK**ORDER * SAMPLES
+
+
+def tile_fast_tucker_taylor_pa_k_kernel(tc, z, G2_words, G2_scales, out):
+    nc = tc.nc
+    with ExitStack() as ctx:
+        ctx.enter_context(tc.manual_schedule())
+        keep = ctx.enter_context(tc.tile_pool(name="keep", bufs=1))
+        piece_pool = ctx.enter_context(tc.tile_pool(name="pieces", bufs=3 * TILES_PER_HALF))
+        grouped_pool = ctx.enter_context(tc.tile_pool(name="grouped", bufs=3))
+        code_pool = ctx.enter_context(tc.tile_pool(name="codes", bufs=3))
+        result_pool = ctx.enter_context(tc.tile_pool(name="results", bufs=2))
+        sums_pool = ctx.enter_context(tc.psum_pool(name="sums", bufs=1))
+        bank_pool = ctx.enter_context(tc.psum_pool(name="banks", bufs=6))
+
+        z_rows = keep.tile([P, SAMPLES], BF16)
+        nc.vector.memset(z_rows[:], 0.0)
+        nc.sync.dma_start(out=z_rows[0 : ORDER * RANK, :], in_=z.rearrange("j r n -> (j r) n"))
+
+        g2_scales = keep.tile([P, PASSES, ROWS], U8, align_bytes=64)
+        nc.vector.memset(g2_scales[:].bitcast(I32), 0)
+        for r in range(4):
+            nc.sync.dma_start(
+                out=g2_scales[r:P:32, :, :].bitcast(I32),
+                in_=G2_scales.rearrange("g (quad r) n -> r quad g n", r=4)[r].bitcast(I32),
+            )
+        g2_words = keep.tile([P, PASSES, ROWS], U32, align_bytes=64)
+        for g in range(0, PASSES, 4):
+            nc.sync.dma_start(
+                out=g2_words[:, g : g + 4, :].bitcast(I32),
+                in_=G2_words[g : g + 4].rearrange("g p n t -> p g (n t)").bitcast(I32),
+            )
+
+        ident_bf16 = keep.tile([P, P], BF16)
+        make_identity(nc, ident_bf16[:])
+        ident_f32 = keep.tile([P, P], F32)
+        make_identity(nc, ident_f32[:])
+
+        z_turned = bank_pool.tile([P, SAMPLE_TILES, P], BF16, tag="bank")
+        for tile_no in range(SAMPLE_TILES):
+            nc.tensor.transpose(
+                z_turned[:, tile_no, :], z_rows[:, tile_no * P : (tile_no + 1) * P], ident_bf16[:]
+            )
+        z_cols = keep.tile([P, SAMPLE_TILES, ORDER * RANK], F32)
+        nc.vector.tensor_copy(out=z_cols[:], in_=z_turned[:, :, 0 : ORDER * RANK])
+
+        hf_scale = keep.tile([P, SAMPLE_TILES, RANK * RANK], F32)
+        nc.vector.tensor_tensor(
+            out=hf_scale[:].rearrange("p j (h f) -> p j h f", h=RANK),
+            in0=z_cols[:, :, 6 * RANK : 7 * RANK].unsqueeze(3).to_broadcast([P, SAMPLE_TILES, RANK, RANK]),
+            in1=z_cols[:, :, 5 * RANK : 6 * RANK].unsqueeze(2).to_broadcast([P, SAMPLE_TILES, RANK, RANK]),
+            op=MULT,
+        )
+
+        ab = keep.tile([P, SAMPLE_TILES, RANK**2], F32)
+        abc = keep.tile([P, SAMPLE_TILES, RANK**3], F32)
+        abcd = keep.tile([P, SAMPLE_TILES, RANK**4], F32)
+        low = keep.tile([P, SAMPLE_TILES, LOW], F32)
+
+        def widen(wide, narrow, factor, tiles):
+            x = narrow.shape[2] // 2
+            for r in range(RANK):
+                column = factor * RANK + r
+                nc.vector.tensor_tensor(
+                    out=wide[:, tiles, :].rearrange("p j (u r x) -> p j u r x", u=2, r=RANK)[:, :, :, r, :],
+                    in0=narrow[:, tiles, :].rearrange("p j (u x) -> p j u x", u=2),
+                    in1=z_cols[:, tiles, column : column + 1]
+                    .unsqueeze(3)
+                    .to_broadcast([P, TILES_PER_HALF, 2, x]),
+                    op=MULT,
+                )
+
+        def prepare(half):
+            first_tile = half * TILES_PER_HALF
+            tiles = slice(first_tile, first_tile + TILES_PER_HALF)
+            widen(ab, z_cols[:, :, 0:RANK], 1, tiles)
+            widen(abc, ab, 2, tiles)
+            widen(abcd, abc, 3, tiles)
+            for tile_no in range(first_tile, first_tile + TILES_PER_HALF):
+                for e in range(RANK):
+                    nc.vector.tensor_scalar(
+                        out=low[:, tile_no, :].rearrange(
+                            "p (eh u el x) -> p eh u el x", eh=2, u=2, el=2
+                        )[:, e // 2, :, e % 2, :],
+                        in0=abcd[:, tile_no, :].rearrange("p (u x) -> p u x", u=2),
+                        scalar1=z_cols[:, tile_no, 4 * RANK + e : 4 * RANK + e + 1],
+                        scalar2=None,
+                        op0=MULT,
+                    )
+
+        pieces = {}
+        grouped = {}
+        codes = {}
+        sums = {}
+
+        def products(step):
+            half, hf = divmod(step, RANK * RANK)
+            pieces[step] = []
+            for i in range(TILES_PER_HALF):
+                tile_no = half * TILES_PER_HALF + i
+                piece = piece_pool.tile([P, LOW], BF16)
+                if (step * TILES_PER_HALF + i) % SCALAR_EVERY == SCALAR_EVERY - 1:
+                    nc.scalar.activation(
+                        out=piece[:], in_=low[:, tile_no, :], func=COPY,
+                        scale=hf_scale[:, tile_no, hf : hf + 1],
+                    )
+                else:
+                    nc.vector.tensor_scalar(
+                        out=piece[:], in0=low[:, tile_no, :],
+                        scalar1=hf_scale[:, tile_no, hf : hf + 1], scalar2=None, op0=MULT,
+                    )
+                pieces[step].append(piece)
+
+        def turn(step):
+            together = grouped_pool.tile([P, 2 * HALF * RANK], BF16, align_bytes=64)
+            pairs = together[:].bitcast(F32).rearrange(
+                "p (eh two i n u) -> p eh two i n u", eh=2, two=2, i=2, u=2
+            )
+            for eh in range(2):
+                for two in range(2):
+                    bank = bank_pool.tile([P, 2, 2, P], F32, tag="bank")
+                    for i in range(2):
+                        piece_pairs = pieces[step][2 * two + i][:].bitcast(F32)
+                        for u in range(2):
+                            first = (2 * eh + u) * P
+                            nc.tensor.transpose(
+                                bank[:, i, u, :], piece_pairs[:, first : first + P], ident_f32[:]
+                            )
+                    nc.scalar.copy(
+                        out=pairs[:, eh, two], in_=bank[:].rearrange("p i u n -> p i n u")
+                    )
+            grouped[step] = together
+
+        def quantise(step):
+            words = code_pool.tile([P, 2 * HALF], U32, align_bytes=64)
+            scales = code_pool.tile([P, 2 * HALF], U8, align_bytes=64)
+            nc.vector.quantize_mx(
+                out=words[:].bitcast(FP8X4), scales=scales[:], in_=grouped[step][:]
+            )
+            codes[step] = (words, scales)
+
+        def multiply(step):
+            half, hf = divmod(step, RANK * RANK)
+            words, scales = codes[step]
+            if hf == 0:
+                for m in range(ROWS // P):
+                    sums[m] = sums_pool.tile([P, HALF], F32, name="sums%d" % m)
+            for eh in range(2):
+                g = 2 * hf + eh
+                columns = slice(eh * HALF, (eh + 1) * HALF)
+                for m in range(ROWS // P):
+                    rows = slice(m * P, (m + 1) * P)
+                    nc.tensor.matmul_mx(
+                        out=sums[m][:],
+                        lhsT=g2_words[:, g, rows].bitcast(FP8X4),
+                        lhsT_scale=g2_scales[:, g, rows],
+                        rhs=words[:, columns].bitcast(FP8X4),
+                        rhs_scale=scales[:, columns],
+                        start=(g == 0),
+                        stop=(g == PASSES - 1),
+                    )
+            if hf == RANK * RANK - 1:
+                for m in range(ROWS // P):
+                    result = result_pool.tile([P, HALF], F32)
+                    if m == 0:
+                        nc.vector.tensor_copy(out=result[:], in_=sums[m][:])
+                    else:
+                        nc.scalar.copy(out=result[:], in_=sums[m][:])
+                    nc.sync.dma_start(
+                        out=out[m * P : (m + 1) * P, half * HALF : (half + 1) * HALF], in_=result[:]
+                    )
+
+        prepare(0)
+        for tick in range(STEPS + 3):
+            if tick < STEPS:
+                products(tick)
+            if tick == STEPS // 4:
+                prepare(1)
+            if 1 <= tick <= STEPS:
+                turn(tick - 1)
+            if 2 <= tick <= STEPS + 1:
+                quantise(tick - 2)
+            if 3 <= tick <= STEPS + 2:
+                multiply(tick - 3)

@@ -22,8 +22,9 @@ SAMPLE_TILES = SAMPLES // P
 HALF = 512
 TILES_PER_HALF = HALF // P
 LOW = RANK**5
-STEPS = 2 * RANK * RANK
-SCALAR_EVERY = 5
+STEPS_PER_HALF = RANK * RANK
+STEPS = 2 * STEPS_PER_HALF
+SCALAR_RESTS = 4
 
 FLOPS = 2 * ROWS * RANK**ORDER * SAMPLES
 
@@ -33,7 +34,7 @@ def tile_fast_tucker_taylor_pa_k_kernel(tc, z, G2_words, G2_scales, out):
     with ExitStack() as ctx:
         ctx.enter_context(tc.manual_schedule())
         keep = ctx.enter_context(tc.tile_pool(name="keep", bufs=1))
-        piece_pool = ctx.enter_context(tc.tile_pool(name="pieces", bufs=3 * TILES_PER_HALF))
+        piece_pool = ctx.enter_context(tc.tile_pool(name="pieces", bufs=2 * TILES_PER_HALF))
         grouped_pool = ctx.enter_context(tc.tile_pool(name="grouped", bufs=3))
         code_pool = ctx.enter_context(tc.tile_pool(name="codes", bufs=3))
         result_pool = ctx.enter_context(tc.tile_pool(name="results", bufs=2))
@@ -71,48 +72,49 @@ def tile_fast_tucker_taylor_pa_k_kernel(tc, z, G2_words, G2_scales, out):
         z_cols = keep.tile([P, SAMPLE_TILES, ORDER * RANK], F32)
         nc.vector.tensor_copy(out=z_cols[:], in_=z_turned[:, :, 0 : ORDER * RANK])
 
-        hf_scale = keep.tile([P, SAMPLE_TILES, RANK * RANK], F32)
-        nc.vector.tensor_tensor(
-            out=hf_scale[:].rearrange("p j (h f) -> p j h f", h=RANK),
-            in0=z_cols[:, :, 6 * RANK : 7 * RANK].unsqueeze(3).to_broadcast([P, SAMPLE_TILES, RANK, RANK]),
-            in1=z_cols[:, :, 5 * RANK : 6 * RANK].unsqueeze(2).to_broadcast([P, SAMPLE_TILES, RANK, RANK]),
-            op=MULT,
-        )
+        def factor(j):
+            return z_cols[:, :, j * RANK : (j + 1) * RANK]
 
-        ab = keep.tile([P, SAMPLE_TILES, RANK**2], F32)
-        abc = keep.tile([P, SAMPLE_TILES, RANK**3], F32)
-        abcd = keep.tile([P, SAMPLE_TILES, RANK**4], F32)
-        low = keep.tile([P, SAMPLE_TILES, LOW], F32)
+        def outer(product, left, right):
+            shape = [P, SAMPLE_TILES, left.shape[2], right.shape[2]]
+            nc.vector.tensor_tensor(
+                out=product.rearrange("p j (x y) -> p j x y", y=right.shape[2]),
+                in0=left.unsqueeze(3).to_broadcast(shape),
+                in1=right.unsqueeze(2).to_broadcast(shape),
+                op=MULT,
+            )
 
-        def widen(wide, narrow, factor, tiles):
-            x = narrow.shape[2] // 2
-            for r in range(RANK):
-                column = factor * RANK + r
-                nc.vector.tensor_tensor(
-                    out=wide[:, tiles, :].rearrange("p j (u r x) -> p j u r x", u=2, r=RANK)[:, :, :, r, :],
-                    in0=narrow[:, tiles, :].rearrange("p j (u x) -> p j u x", u=2),
-                    in1=z_cols[:, tiles, column : column + 1]
-                    .unsqueeze(3)
-                    .to_broadcast([P, TILES_PER_HALF, 2, x]),
-                    op=MULT,
+        def times_column(on_scalar, product, values, column):
+            if on_scalar:
+                nc.scalar.activation(out=product, in_=values, func=COPY, scale=column)
+            else:
+                nc.vector.tensor_scalar(
+                    out=product, in0=values, scalar1=column, scalar2=None, op0=MULT
                 )
 
+        ab = keep.tile([P, SAMPLE_TILES, 2, 2 * RANK], F32)
+        dc = keep.tile([P, SAMPLE_TILES, RANK * RANK], F32)
+        abcd = keep.tile([P, SAMPLE_TILES, 2, P], F32)
+        hf_scale = keep.tile([P, SAMPLE_TILES, STEPS_PER_HALF], F32)
+        for u in range(2):
+            outer(ab[:, :, u, :], factor(1), factor(0)[:, :, 2 * u : 2 * u + 2])
+        outer(dc[:], factor(3), factor(2))
+        for u in range(2):
+            outer(abcd[:, :, u, :], dc[:], ab[:, :, u, :])
+        outer(hf_scale[:], factor(6), factor(5))
+
+        low = keep.tile([P, SAMPLE_TILES, LOW], F32)
+
         def prepare(half):
-            first_tile = half * TILES_PER_HALF
-            tiles = slice(first_tile, first_tile + TILES_PER_HALF)
-            widen(ab, z_cols[:, :, 0:RANK], 1, tiles)
-            widen(abc, ab, 2, tiles)
-            widen(abcd, abc, 3, tiles)
-            for tile_no in range(first_tile, first_tile + TILES_PER_HALF):
+            for i in range(TILES_PER_HALF):
+                tile_no = half * TILES_PER_HALF + i
+                by_e = low[:, tile_no, :].rearrange("p (eh u el x) -> p eh u el x", eh=2, u=2, el=2)
                 for e in range(RANK):
-                    nc.vector.tensor_scalar(
-                        out=low[:, tile_no, :].rearrange(
-                            "p (eh u el x) -> p eh u el x", eh=2, u=2, el=2
-                        )[:, e // 2, :, e % 2, :],
-                        in0=abcd[:, tile_no, :].rearrange("p (u x) -> p u x", u=2),
-                        scalar1=z_cols[:, tile_no, 4 * RANK + e : 4 * RANK + e + 1],
-                        scalar2=None,
-                        op0=MULT,
+                    times_column(
+                        i >= TILES_PER_HALF // 2,
+                        by_e[:, e // 2, :, e % 2, :],
+                        abcd[:, tile_no],
+                        z_cols[:, tile_no, 4 * RANK + e : 4 * RANK + e + 1],
                     )
 
         pieces = {}
@@ -121,21 +123,17 @@ def tile_fast_tucker_taylor_pa_k_kernel(tc, z, G2_words, G2_scales, out):
         sums = {}
 
         def products(step):
-            half, hf = divmod(step, RANK * RANK)
+            half, hf = divmod(step, STEPS_PER_HALF)
             pieces[step] = []
             for i in range(TILES_PER_HALF):
                 tile_no = half * TILES_PER_HALF + i
                 piece = piece_pool.tile([P, LOW], BF16)
-                if (step * TILES_PER_HALF + i) % SCALAR_EVERY == SCALAR_EVERY - 1:
-                    nc.scalar.activation(
-                        out=piece[:], in_=low[:, tile_no, :], func=COPY,
-                        scale=hf_scale[:, tile_no, hf : hf + 1],
-                    )
-                else:
-                    nc.vector.tensor_scalar(
-                        out=piece[:], in0=low[:, tile_no, :],
-                        scalar1=hf_scale[:, tile_no, hf : hf + 1], scalar2=None, op0=MULT,
-                    )
+                times_column(
+                    i == TILES_PER_HALF - 1 and step % SCALAR_RESTS != 0,
+                    piece[:],
+                    low[:, tile_no, :],
+                    hf_scale[:, tile_no, hf : hf + 1],
+                )
                 pieces[step].append(piece)
 
         def turn(step):
@@ -143,8 +141,8 @@ def tile_fast_tucker_taylor_pa_k_kernel(tc, z, G2_words, G2_scales, out):
             pairs = together[:].bitcast(F32).rearrange(
                 "p (eh two i n u) -> p eh two i n u", eh=2, two=2, i=2, u=2
             )
-            for eh in range(2):
-                for two in range(2):
+            for two in range(2):
+                for eh in range(2):
                     bank = bank_pool.tile([P, 2, 2, P], F32, tag="bank")
                     for i in range(2):
                         piece_pairs = pieces[step][2 * two + i][:].bitcast(F32)
@@ -167,7 +165,7 @@ def tile_fast_tucker_taylor_pa_k_kernel(tc, z, G2_words, G2_scales, out):
             codes[step] = (words, scales)
 
         def multiply(step):
-            half, hf = divmod(step, RANK * RANK)
+            hf = step % STEPS_PER_HALF
             words, scales = codes[step]
             if hf == 0:
                 for m in range(ROWS // P):
@@ -186,26 +184,27 @@ def tile_fast_tucker_taylor_pa_k_kernel(tc, z, G2_words, G2_scales, out):
                         start=(g == 0),
                         stop=(g == PASSES - 1),
                     )
-            if hf == RANK * RANK - 1:
-                for m in range(ROWS // P):
-                    result = result_pool.tile([P, HALF], F32)
-                    if m == 0:
-                        nc.vector.tensor_copy(out=result[:], in_=sums[m][:])
-                    else:
-                        nc.scalar.copy(out=result[:], in_=sums[m][:])
-                    nc.sync.dma_start(
-                        out=out[m * P : (m + 1) * P, half * HALF : (half + 1) * HALF], in_=result[:]
-                    )
+
+        def store(half):
+            for m in range(ROWS // P):
+                result = result_pool.tile([P, HALF], F32)
+                if m == 0:
+                    nc.vector.tensor_copy(out=result[:], in_=sums[m][:])
+                else:
+                    nc.scalar.copy(out=result[:], in_=sums[m][:])
+                nc.sync.dma_start(
+                    out=out[m * P : (m + 1) * P, half * HALF : (half + 1) * HALF], in_=result[:]
+                )
 
         prepare(0)
-        for tick in range(STEPS + 3):
+        for tick in range(STEPS + 2):
             if tick < STEPS:
                 products(tick)
-            if tick == STEPS // 4:
+                turn(tick)
+            if tick == STEPS_PER_HALF // 2:
                 prepare(1)
+            if tick >= 2 and (tick - 2) % STEPS_PER_HALF == STEPS_PER_HALF - 1:
+                store((tick - 2) // STEPS_PER_HALF)
             if 1 <= tick <= STEPS:
-                turn(tick - 1)
-            if 2 <= tick <= STEPS + 1:
-                quantise(tick - 2)
-            if 3 <= tick <= STEPS + 2:
-                multiply(tick - 3)
+                quantise(tick - 1)
+                multiply(tick - 1)

@@ -24,7 +24,7 @@ TILES_PER_HALF = HALF // P
 LOW = RANK**5
 STEPS_PER_HALF = RANK * RANK
 STEPS = 2 * STEPS_PER_HALF
-SCALAR_RESTS = 4
+SCALAR_RESTS = 3
 
 FLOPS = 2 * ROWS * RANK**ORDER * SAMPLES
 
@@ -34,7 +34,7 @@ def tile_fast_tucker_taylor_pa_k_kernel(tc, z, G2_words, G2_scales, out):
     with ExitStack() as ctx:
         ctx.enter_context(tc.manual_schedule())
         keep = ctx.enter_context(tc.tile_pool(name="keep", bufs=1))
-        piece_pool = ctx.enter_context(tc.tile_pool(name="pieces", bufs=2 * TILES_PER_HALF))
+        piece_pool = ctx.enter_context(tc.tile_pool(name="pieces", bufs=3 * TILES_PER_HALF))
         grouped_pool = ctx.enter_context(tc.tile_pool(name="grouped", bufs=3))
         code_pool = ctx.enter_context(tc.tile_pool(name="codes", bufs=3))
         result_pool = ctx.enter_context(tc.tile_pool(name="results", bufs=2))
@@ -76,7 +76,7 @@ def tile_fast_tucker_taylor_pa_k_kernel(tc, z, G2_words, G2_scales, out):
             return z_cols[:, :, j * RANK : (j + 1) * RANK]
 
         def outer(product, left, right):
-            shape = [P, SAMPLE_TILES, left.shape[2], right.shape[2]]
+            shape = [P, left.shape[1], left.shape[2], right.shape[2]]
             nc.vector.tensor_tensor(
                 out=product.rearrange("p j (x y) -> p j x y", y=right.shape[2]),
                 in0=left.unsqueeze(3).to_broadcast(shape),
@@ -99,13 +99,14 @@ def tile_fast_tucker_taylor_pa_k_kernel(tc, z, G2_words, G2_scales, out):
         for u in range(2):
             outer(ab[:, :, u, :], factor(1), factor(0)[:, :, 2 * u : 2 * u + 2])
         outer(dc[:], factor(3), factor(2))
-        for u in range(2):
-            outer(abcd[:, :, u, :], dc[:], ab[:, :, u, :])
         outer(hf_scale[:], factor(6), factor(5))
 
         low = keep.tile([P, SAMPLE_TILES, LOW], F32)
 
         def prepare(half):
+            tiles = slice(half * TILES_PER_HALF, (half + 1) * TILES_PER_HALF)
+            for u in range(2):
+                outer(abcd[:, tiles, u, :], dc[:, tiles, :], ab[:, tiles, u, :])
             for i in range(TILES_PER_HALF):
                 tile_no = half * TILES_PER_HALF + i
                 by_e = low[:, tile_no, :].rearrange("p (eh u el x) -> p eh u el x", eh=2, u=2, el=2)
@@ -136,25 +137,23 @@ def tile_fast_tucker_taylor_pa_k_kernel(tc, z, G2_words, G2_scales, out):
                 )
                 pieces[step].append(piece)
 
-        def turn(step):
-            together = grouped_pool.tile([P, 2 * HALF * RANK], BF16, align_bytes=64)
-            pairs = together[:].bitcast(F32).rearrange(
+        def turn(step, eh):
+            if eh == 0:
+                together = grouped_pool.tile([P, 2 * HALF * RANK], BF16, align_bytes=64)
+                grouped[step] = together
+            pairs = grouped[step][:].bitcast(F32).rearrange(
                 "p (eh two i n u) -> p eh two i n u", eh=2, two=2, i=2, u=2
             )
             for two in range(2):
-                for eh in range(2):
-                    bank = bank_pool.tile([P, 2, 2, P], F32, tag="bank")
-                    for i in range(2):
-                        piece_pairs = pieces[step][2 * two + i][:].bitcast(F32)
-                        for u in range(2):
-                            first = (2 * eh + u) * P
-                            nc.tensor.transpose(
-                                bank[:, i, u, :], piece_pairs[:, first : first + P], ident_f32[:]
-                            )
-                    nc.scalar.copy(
-                        out=pairs[:, eh, two], in_=bank[:].rearrange("p i u n -> p i n u")
-                    )
-            grouped[step] = together
+                bank = bank_pool.tile([P, 2, 2, P], F32, tag="bank")
+                for i in range(2):
+                    piece_pairs = pieces[step][2 * two + i][:].bitcast(F32)
+                    for u in range(2):
+                        first = (2 * eh + u) * P
+                        nc.tensor.transpose(
+                            bank[:, i, u, :], piece_pairs[:, first : first + P], ident_f32[:]
+                        )
+                nc.scalar.copy(out=pairs[:, eh, two], in_=bank[:].rearrange("p i u n -> p i n u"))
 
         def quantise(step):
             words = code_pool.tile([P, 2 * HALF], U32, align_bytes=64)
@@ -164,26 +163,24 @@ def tile_fast_tucker_taylor_pa_k_kernel(tc, z, G2_words, G2_scales, out):
             )
             codes[step] = (words, scales)
 
-        def multiply(step):
-            hf = step % STEPS_PER_HALF
+        def multiply(step, eh):
+            g = 2 * (step % STEPS_PER_HALF) + eh
             words, scales = codes[step]
-            if hf == 0:
+            if g == 0:
                 for m in range(ROWS // P):
                     sums[m] = sums_pool.tile([P, HALF], F32, name="sums%d" % m)
-            for eh in range(2):
-                g = 2 * hf + eh
-                columns = slice(eh * HALF, (eh + 1) * HALF)
-                for m in range(ROWS // P):
-                    rows = slice(m * P, (m + 1) * P)
-                    nc.tensor.matmul_mx(
-                        out=sums[m][:],
-                        lhsT=g2_words[:, g, rows].bitcast(FP8X4),
-                        lhsT_scale=g2_scales[:, g, rows],
-                        rhs=words[:, columns].bitcast(FP8X4),
-                        rhs_scale=scales[:, columns],
-                        start=(g == 0),
-                        stop=(g == PASSES - 1),
-                    )
+            columns = slice(eh * HALF, (eh + 1) * HALF)
+            for m in range(ROWS // P):
+                rows = slice(m * P, (m + 1) * P)
+                nc.tensor.matmul_mx(
+                    out=sums[m][:],
+                    lhsT=g2_words[:, g, rows].bitcast(FP8X4),
+                    lhsT_scale=g2_scales[:, g, rows],
+                    rhs=words[:, columns].bitcast(FP8X4),
+                    rhs_scale=scales[:, columns],
+                    start=(g == 0),
+                    stop=(g == PASSES - 1),
+                )
 
         def store(half):
             for m in range(ROWS // P):
@@ -197,14 +194,17 @@ def tile_fast_tucker_taylor_pa_k_kernel(tc, z, G2_words, G2_scales, out):
                 )
 
         prepare(0)
-        for tick in range(STEPS + 2):
+        for tick in range(STEPS + 3):
             if tick < STEPS:
                 products(tick)
-                turn(tick)
             if tick == STEPS_PER_HALF // 2:
                 prepare(1)
-            if tick >= 2 and (tick - 2) % STEPS_PER_HALF == STEPS_PER_HALF - 1:
-                store((tick - 2) // STEPS_PER_HALF)
-            if 1 <= tick <= STEPS:
-                quantise(tick - 1)
-                multiply(tick - 1)
+            for eh in range(2):
+                if 1 <= tick <= STEPS:
+                    turn(tick - 1, eh)
+                if 3 <= tick:
+                    multiply(tick - 3, eh)
+            if 2 <= tick <= STEPS + 1:
+                quantise(tick - 2)
+            if 3 <= tick and (tick - 3) % STEPS_PER_HALF == STEPS_PER_HALF - 1:
+                store((tick - 3) // STEPS_PER_HALF)

@@ -199,10 +199,11 @@ def tile_fast_tucker_taylor_pa_k_kernel(tc, z, G2_words, G2_scales, out):
                 products(tick)
             if tick == STEPS_PER_HALF // 2:
                 prepare(1)
-            for eh in range(2):
-                if 1 <= tick <= STEPS:
+            if 1 <= tick <= STEPS:
+                for eh in range(2):
                     turn(tick - 1, eh)
-                if 3 <= tick:
+            if 3 <= tick:
+                for eh in range(2):
                     multiply(tick - 3, eh)
             if 2 <= tick <= STEPS + 1:
                 quantise(tick - 2)

@@ -24,7 +24,7 @@ TILES_PER_HALF = HALF // P
 LOW = RANK**5
 STEPS_PER_HALF = RANK * RANK
 STEPS = 2 * STEPS_PER_HALF
-SCALAR_RESTS = 3
+SCALAR_COLUMNS = 704
 
 FLOPS = 2 * ROWS * RANK**ORDER * SAMPLES
 
@@ -129,10 +129,19 @@ def tile_fast_tucker_taylor_pa_k_kernel(tc, z, G2_words, G2_scales, out):
             for i in range(TILES_PER_HALF):
                 tile_no = half * TILES_PER_HALF + i
                 piece = piece_pool.tile([P, LOW], BF16)
+                by_vector = LOW
+                if i == TILES_PER_HALF - 1:
+                    by_vector -= SCALAR_COLUMNS
+                    times_column(
+                        True,
+                        piece[:, by_vector:],
+                        low[:, tile_no, by_vector:],
+                        hf_scale[:, tile_no, hf : hf + 1],
+                    )
                 times_column(
-                    i == TILES_PER_HALF - 1 and step % SCALAR_RESTS != 0,
-                    piece[:],
-                    low[:, tile_no, :],
+                    False,
+                    piece[:, 0:by_vector],
+                    low[:, tile_no, 0:by_vector],
                     hf_scale[:, tile_no, hf : hf + 1],
                 )
                 pieces[step].append(piece)

@@ -10,6 +10,7 @@ U32 = mybir.dt.uint32
 U8 = mybir.dt.uint8
 FP8X4 = mybir.dt.float8_e4m3fn_x4
 MULT = mybir.AluOpType.mult
+ADD = mybir.AluOpType.add
 COPY = mybir.ActivationFunctionType.Copy
 
 P = 128
@@ -24,7 +25,11 @@ TILES_PER_HALF = HALF // P
 LOW = RANK**5
 STEPS_PER_HALF = RANK * RANK
 STEPS = 2 * STEPS_PER_HALF
-SCALAR_COLUMNS = 704
+BY_GPSIMD, BY_VECTOR, BY_SCALAR, ROAD_B = range(4)
+TURNED_TILES = 3
+Y_STEPS = 4
+REUSE = 3
+PREPARE_TICK = 8
 
 FLOPS = 2 * ROWS * RANK**ORDER * SAMPLES
 
@@ -34,19 +39,24 @@ def tile_fast_tucker_taylor_pa_k_kernel(tc, z, G2_words, G2_scales, out):
     with ExitStack() as ctx:
         ctx.enter_context(tc.manual_schedule())
         keep = ctx.enter_context(tc.tile_pool(name="keep", bufs=1))
-        piece_pool = ctx.enter_context(tc.tile_pool(name="pieces", bufs=3 * TILES_PER_HALF))
-        grouped_pool = ctx.enter_context(tc.tile_pool(name="grouped", bufs=3))
+        piece_pool = ctx.enter_context(tc.tile_pool(name="pieces", bufs=3))
+        grouped_pool = ctx.enter_context(tc.tile_pool(name="grouped", bufs=REUSE + 2))
         code_pool = ctx.enter_context(tc.tile_pool(name="codes", bufs=3))
         result_pool = ctx.enter_context(tc.tile_pool(name="results", bufs=2))
         sums_pool = ctx.enter_context(tc.psum_pool(name="sums", bufs=1))
-        bank_pool = ctx.enter_context(tc.psum_pool(name="banks", bufs=6))
+        y_pool = ctx.enter_context(tc.psum_pool(name="y", bufs=2))
+        bank_pool = ctx.enter_context(tc.psum_pool(name="banks", bufs=4))
 
+        ident_bf16 = keep.tile([P, P], BF16)
+        make_identity(nc, ident_bf16[:])
         z_rows = keep.tile([P, SAMPLES], BF16)
-        nc.vector.memset(z_rows[:], 0.0)
         nc.sync.dma_start(out=z_rows[0 : ORDER * RANK, :], in_=z.rearrange("j r n -> (j r) n"))
+        nc.sync.dma_start(out=z_rows[ORDER * RANK : 32, :], in_=z[0])
+        nc.vector.memset(z_rows[32:64, :].bitcast(I32), 0)
+        nc.vector.memset(z_rows[64:P, :].bitcast(I32), 0)
 
         g2_scales = keep.tile([P, PASSES, ROWS], U8, align_bytes=64)
-        nc.vector.memset(g2_scales[:].bitcast(I32), 0)
+        nc.gpsimd.memset(g2_scales[:].bitcast(I32), 0)
         for r in range(4):
             nc.sync.dma_start(
                 out=g2_scales[r:P:32, :, :].bitcast(I32),
@@ -59,8 +69,6 @@ def tile_fast_tucker_taylor_pa_k_kernel(tc, z, G2_words, G2_scales, out):
                 in_=G2_words[g : g + 4].rearrange("g p n t -> p g (n t)").bitcast(I32),
             )
 
-        ident_bf16 = keep.tile([P, P], BF16)
-        make_identity(nc, ident_bf16[:])
         ident_f32 = keep.tile([P, P], F32)
         make_identity(nc, ident_f32[:])
 
@@ -103,66 +111,112 @@ def tile_fast_tucker_taylor_pa_k_kernel(tc, z, G2_words, G2_scales, out):
 
         low = keep.tile([P, SAMPLE_TILES, LOW], F32)
 
-        def prepare(half):
+        def make_abcd(half):
             tiles = slice(half * TILES_PER_HALF, (half + 1) * TILES_PER_HALF)
             for u in range(2):
                 outer(abcd[:, tiles, u, :], dc[:, tiles, :], ab[:, tiles, u, :])
-            for i in range(TILES_PER_HALF):
-                tile_no = half * TILES_PER_HALF + i
-                by_e = low[:, tile_no, :].rearrange("p (eh u el x) -> p eh u el x", eh=2, u=2, el=2)
-                for e in range(RANK):
-                    times_column(
-                        i >= TILES_PER_HALF // 2,
-                        by_e[:, e // 2, :, e % 2, :],
-                        abcd[:, tile_no],
-                        z_cols[:, tile_no, 4 * RANK + e : 4 * RANK + e + 1],
-                    )
+
+        def make_low(tile_no, e, on_scalar):
+            by_e = low[:, tile_no, :].rearrange("p (eh u el x) -> p eh u el x", eh=2, u=2, el=2)
+            times_column(
+                on_scalar,
+                by_e[:, e // 2, :, e % 2, :],
+                abcd[:, tile_no],
+                z_cols[:, tile_no, 4 * RANK + e : 4 * RANK + e + 1],
+            )
 
         pieces = {}
         grouped = {}
         codes = {}
         sums = {}
+        x_turned = {}
+        y_turned = {}
 
-        def products(step):
+        def gpsimd_product(step):
             half, hf = divmod(step, STEPS_PER_HALF)
-            pieces[step] = []
-            for i in range(TILES_PER_HALF):
-                tile_no = half * TILES_PER_HALF + i
-                piece = piece_pool.tile([P, LOW], BF16)
-                by_vector = LOW
-                if i == TILES_PER_HALF - 1:
-                    by_vector -= SCALAR_COLUMNS
-                    times_column(
-                        True,
-                        piece[:, by_vector:],
-                        low[:, tile_no, by_vector:],
-                        hf_scale[:, tile_no, hf : hf + 1],
-                    )
-                times_column(
-                    False,
-                    piece[:, 0:by_vector],
-                    low[:, tile_no, 0:by_vector],
-                    hf_scale[:, tile_no, hf : hf + 1],
-                )
-                pieces[step].append(piece)
+            tile_no = half * TILES_PER_HALF + BY_GPSIMD
+            if step < REUSE:
+                first = keep.tile([P, LOW], BF16, name="first%d" % step)
+                piece = first[:]
+            else:
+                piece = grouped[step - REUSE][:, 0:LOW]
+            nc.gpsimd.tensor_scalar(
+                out=piece,
+                in0=low[:, tile_no, :],
+                scalar1=hf_scale[:, tile_no, hf : hf + 1],
+                scalar2=0.0,
+                op0=MULT,
+                op1=ADD,
+            )
+            pieces[step, BY_GPSIMD] = piece
 
-        def turn(step, eh):
-            if eh == 0:
+        def product(step, i):
+            half, hf = divmod(step, STEPS_PER_HALF)
+            tile_no = half * TILES_PER_HALF + i
+            piece = piece_pool.tile([P, LOW], BF16, name="piece%d" % i)
+            times_column(
+                i == BY_SCALAR, piece[:], low[:, tile_no, :], hf_scale[:, tile_no, hf : hf + 1]
+            )
+            pieces[step, i] = piece[:]
+
+        def grouped_tile(step):
+            if step not in grouped:
                 together = grouped_pool.tile([P, 2 * HALF * RANK], BF16, align_bytes=64)
                 grouped[step] = together
-            pairs = grouped[step][:].bitcast(F32).rearrange(
-                "p (eh two i n u) -> p eh two i n u", eh=2, two=2, i=2, u=2
+            return grouped[step]
+
+        def turn(step):
+            pairs = grouped_tile(step)[:].bitcast(F32).rearrange(
+                "p (eh i n u) -> p eh i n u", eh=2, i=TILES_PER_HALF, u=2
             )
-            for two in range(2):
+            for i in range(TURNED_TILES):
                 bank = bank_pool.tile([P, 2, 2, P], F32, tag="bank")
-                for i in range(2):
-                    piece_pairs = pieces[step][2 * two + i][:].bitcast(F32)
+                piece_pairs = pieces[step, i].bitcast(F32)
+                for eh in range(2):
                     for u in range(2):
                         first = (2 * eh + u) * P
                         nc.tensor.transpose(
-                            bank[:, i, u, :], piece_pairs[:, first : first + P], ident_f32[:]
+                            bank[:, eh, u, :], piece_pairs[:, first : first + P], ident_f32[:]
                         )
-                nc.scalar.copy(out=pairs[:, eh, two], in_=bank[:].rearrange("p i u n -> p i n u"))
+                nc.scalar.copy(out=pairs[:, :, i], in_=bank[:].rearrange("p e u n -> p e n u"))
+
+        def turn_low(half):
+            tile_no = half * TILES_PER_HALF + ROAD_B
+            x = keep.tile([P, 2, P, RANK], F32, name="x%d" % half)
+            for eh in range(2):
+                bank = bank_pool.tile([P, RANK, P], F32, tag="bank")
+                for a in range(RANK):
+                    first = (2 * eh + a // 2) * 2 * P + a % 2
+                    nc.tensor.transpose(
+                        bank[:, a, :], low[:, tile_no, first : first + 2 * P - 1 : 2], ident_f32[:]
+                    )
+                nc.scalar.copy(out=x[:, eh], in_=bank[:].rearrange("p a n -> p n a"))
+            x_turned[half] = x
+
+        def turn_scales(group):
+            y = y_pool.tile([P, Y_STEPS, P], F32)
+            for j in range(Y_STEPS):
+                half, hf = divmod(Y_STEPS * group + j, STEPS_PER_HALF)
+                tile_no = half * TILES_PER_HALF + ROAD_B
+                nc.tensor.transpose(
+                    y[:, j, :],
+                    hf_scale[:, tile_no, hf : hf + 1].to_broadcast([P, P]),
+                    ident_f32[:],
+                )
+            y_turned[group] = y
+
+        def product_b(step):
+            shape = [P, 2, P, RANK]
+            columns = grouped_tile(step)[:].rearrange(
+                "p (eh i n a) -> p eh i n a", eh=2, i=TILES_PER_HALF, a=RANK
+            )[:, :, ROAD_B]
+            y = y_turned[step // Y_STEPS][:, step % Y_STEPS, :]
+            nc.vector.tensor_tensor(
+                out=columns,
+                in0=x_turned[step // STEPS_PER_HALF][:],
+                in1=y.unsqueeze(1).unsqueeze(3).to_broadcast(shape),
+                op=MULT,
+            )
 
         def quantise(step):
             words = code_pool.tile([P, 2 * HALF], U32, align_bytes=64)
@@ -202,19 +256,37 @@ def tile_fast_tucker_taylor_pa_k_kernel(tc, z, G2_words, G2_scales, out):
                     out=out[m * P : (m + 1) * P, half * HALF : (half + 1) * HALF], in_=result[:]
                 )
 
-        prepare(0)
+        make_abcd(0)
+        for i in range(TILES_PER_HALF):
+            for e in range(RANK):
+                make_low(i, e, on_scalar=i >= TILES_PER_HALF // 2)
+        gpsimd_product(0)
+        turn_scales(0)
+        turn_low(0)
         for tick in range(STEPS + 3):
+            if tick >= 4 and (tick - 4) % STEPS_PER_HALF == STEPS_PER_HALF - 1:
+                store((tick - 4) // STEPS_PER_HALF)
             if tick < STEPS:
-                products(tick)
-            if tick == STEPS_PER_HALF // 2:
-                prepare(1)
+                product(tick, BY_VECTOR)
+                product(tick, BY_SCALAR)
+            if tick == PREPARE_TICK:
+                make_abcd(1)
+            if PREPARE_TICK < tick <= PREPARE_TICK + TILES_PER_HALF:
+                tile_no = TILES_PER_HALF + tick - PREPARE_TICK - 1
+                for e in range(RANK):
+                    make_low(tile_no, e, on_scalar=e >= RANK // 2)
+            if 2 <= tick <= STEPS + 1:
+                quantise(tick - 2)
+            if tick + 1 < STEPS:
+                gpsimd_product(tick + 1)
+            if tick % Y_STEPS == 1 and tick + Y_STEPS < STEPS:
+                turn_scales(tick // Y_STEPS + 1)
             if 1 <= tick <= STEPS:
-                for eh in range(2):
-                    turn(tick - 1, eh)
+                product_b(tick - 1)
+                turn(tick - 1)
+            if tick == PREPARE_TICK + TILES_PER_HALF + 1:
+                turn_low(1)
             if 3 <= tick:
                 for eh in range(2):
                     multiply(tick - 3, eh)
-            if 2 <= tick <= STEPS + 1:
-                quantise(tick - 2)
-            if 3 <= tick and (tick - 3) % STEPS_PER_HALF == STEPS_PER_HALF - 1:
-                store((tick - 3) // STEPS_PER_HALF)
+        store(1)

@@ -25,10 +25,11 @@ TILES_PER_HALF = HALF // P
 LOW = RANK**5
 STEPS_PER_HALF = RANK * RANK
 STEPS = 2 * STEPS_PER_HALF
+GPSIMD_COLUMNS = 896
 BY_GPSIMD, BY_VECTOR, BY_SCALAR, ROAD_B = range(4)
 TURNED_TILES = 3
 Y_STEPS = 4
-REUSE = 3
+REUSE = 4
 PREPARE_TICK = 8
 
 FLOPS = 2 * ROWS * RANK**ORDER * SAMPLES
@@ -141,14 +142,24 @@ def tile_fast_tucker_taylor_pa_k_kernel(tc, z, G2_words, G2_scales, out):
             else:
                 piece = grouped[step - REUSE][:, 0:LOW]
             nc.gpsimd.tensor_scalar(
-                out=piece,
-                in0=low[:, tile_no, :],
+                out=piece[:, 0:GPSIMD_COLUMNS],
+                in0=low[:, tile_no, 0:GPSIMD_COLUMNS],
                 scalar1=hf_scale[:, tile_no, hf : hf + 1],
                 scalar2=0.0,
                 op0=MULT,
                 op1=ADD,
             )
             pieces[step, BY_GPSIMD] = piece
+
+        def finish_gpsimd_product(step):
+            half, hf = divmod(step, STEPS_PER_HALF)
+            tile_no = half * TILES_PER_HALF + BY_GPSIMD
+            times_column(
+                True,
+                pieces[step, BY_GPSIMD][:, GPSIMD_COLUMNS:],
+                low[:, tile_no, GPSIMD_COLUMNS:],
+                hf_scale[:, tile_no, hf : hf + 1],
+            )
 
         def product(step, i):
             half, hf = divmod(step, STEPS_PER_HALF)
@@ -257,26 +268,27 @@ def tile_fast_tucker_taylor_pa_k_kernel(tc, z, G2_words, G2_scales, out):
                 )
 
         make_abcd(0)
-        for i in range(TILES_PER_HALF):
+        for i in (BY_VECTOR, BY_GPSIMD, BY_SCALAR, ROAD_B):
             for e in range(RANK):
-                make_low(i, e, on_scalar=i >= TILES_PER_HALF // 2)
+                make_low(i, e, on_scalar=i in (BY_SCALAR, ROAD_B))
         gpsimd_product(0)
         turn_scales(0)
         turn_low(0)
-        for tick in range(STEPS + 3):
-            if tick >= 4 and (tick - 4) % STEPS_PER_HALF == STEPS_PER_HALF - 1:
-                store((tick - 4) // STEPS_PER_HALF)
-            if tick < STEPS:
-                product(tick, BY_VECTOR)
-                product(tick, BY_SCALAR)
+        for tick in range(STEPS + 4):
+            if tick == STEPS_PER_HALF + 4:
+                store(0)
             if tick == PREPARE_TICK:
                 make_abcd(1)
             if PREPARE_TICK < tick <= PREPARE_TICK + TILES_PER_HALF:
                 tile_no = TILES_PER_HALF + tick - PREPARE_TICK - 1
                 for e in range(RANK):
                     make_low(tile_no, e, on_scalar=e >= RANK // 2)
-            if 2 <= tick <= STEPS + 1:
-                quantise(tick - 2)
+            if 3 <= tick <= STEPS + 2:
+                quantise(tick - 3)
+            if tick < STEPS:
+                product(tick, BY_VECTOR)
+                product(tick, BY_SCALAR)
+                finish_gpsimd_product(tick)
             if tick + 1 < STEPS:
                 gpsimd_product(tick + 1)
             if tick % Y_STEPS == 1 and tick + Y_STEPS < STEPS:
@@ -286,7 +298,7 @@ def tile_fast_tucker_taylor_pa_k_kernel(tc, z, G2_words, G2_scales, out):
                 turn(tick - 1)
             if tick == PREPARE_TICK + TILES_PER_HALF + 1:
                 turn_low(1)
-            if 3 <= tick:
+            if 4 <= tick:
                 for eh in range(2):
-                    multiply(tick - 3, eh)
+                    multiply(tick - 4, eh)
         store(1)

@@ -25,12 +25,15 @@ TILES_PER_HALF = HALF // P
 LOW = RANK**5
 STEPS_PER_HALF = RANK * RANK
 STEPS = 2 * STEPS_PER_HALF
-GPSIMD_COLUMNS = 896
 BY_GPSIMD, BY_VECTOR, BY_SCALAR, ROAD_B = range(4)
 TURNED_TILES = 3
+PAIR = 2
+GPSIMD_COLUMNS = 864
+GPSIMD_STARTS = 2 * PAIR
 Y_STEPS = 4
-REUSE = 4
-PREPARE_TICK = 8
+QUANTISE_LAG = 2 * PAIR
+MULTIPLY_LAG = QUANTISE_LAG + 1
+PREPARE_PAIR = 3
 
 FLOPS = 2 * ROWS * RANK**ORDER * SAMPLES
 
@@ -40,8 +43,8 @@ def tile_fast_tucker_taylor_pa_k_kernel(tc, z, G2_words, G2_scales, out):
     with ExitStack() as ctx:
         ctx.enter_context(tc.manual_schedule())
         keep = ctx.enter_context(tc.tile_pool(name="keep", bufs=1))
-        piece_pool = ctx.enter_context(tc.tile_pool(name="pieces", bufs=3))
-        grouped_pool = ctx.enter_context(tc.tile_pool(name="grouped", bufs=REUSE + 2))
+        piece_pool = ctx.enter_context(tc.tile_pool(name="pieces", bufs=2 * PAIR))
+        grouped_pool = ctx.enter_context(tc.tile_pool(name="grouped", bufs=4 * PAIR))
         code_pool = ctx.enter_context(tc.tile_pool(name="codes", bufs=3))
         result_pool = ctx.enter_context(tc.tile_pool(name="results", bufs=2))
         sums_pool = ctx.enter_context(tc.psum_pool(name="sums", bufs=1))
@@ -57,7 +60,7 @@ def tile_fast_tucker_taylor_pa_k_kernel(tc, z, G2_words, G2_scales, out):
         nc.vector.memset(z_rows[64:P, :].bitcast(I32), 0)
 
         g2_scales = keep.tile([P, PASSES, ROWS], U8, align_bytes=64)
-        nc.gpsimd.memset(g2_scales[:].bitcast(I32), 0)
+        nc.vector.memset(g2_scales[:].bitcast(I32), 0)
         for r in range(4):
             nc.sync.dma_start(
                 out=g2_scales[r:P:32, :, :].bitcast(I32),
@@ -73,16 +76,25 @@ def tile_fast_tucker_taylor_pa_k_kernel(tc, z, G2_words, G2_scales, out):
         ident_f32 = keep.tile([P, P], F32)
         make_identity(nc, ident_f32[:])
 
-        z_turned = bank_pool.tile([P, SAMPLE_TILES, P], BF16, tag="bank")
-        for tile_no in range(SAMPLE_TILES):
-            nc.tensor.transpose(
-                z_turned[:, tile_no, :], z_rows[:, tile_no * P : (tile_no + 1) * P], ident_bf16[:]
-            )
         z_cols = keep.tile([P, SAMPLE_TILES, ORDER * RANK], F32)
-        nc.vector.tensor_copy(out=z_cols[:], in_=z_turned[:, :, 0 : ORDER * RANK])
+        z_turned = {}
 
-        def factor(j):
-            return z_cols[:, :, j * RANK : (j + 1) * RANK]
+        def turn_z(half):
+            z_bank = bank_pool.tile([P, TILES_PER_HALF, P], BF16, tag="bank")
+            for i in range(TILES_PER_HALF):
+                tile_no = half * TILES_PER_HALF + i
+                nc.tensor.transpose(
+                    z_bank[:, i, :], z_rows[:, tile_no * P : (tile_no + 1) * P], ident_bf16[:]
+                )
+            z_turned[half] = z_bank
+
+        def tiles_of(half):
+            return slice(half * TILES_PER_HALF, (half + 1) * TILES_PER_HALF)
+
+        def keep_z(half):
+            nc.vector.tensor_copy(
+                out=z_cols[:, tiles_of(half), :], in_=z_turned[half][:, :, 0 : ORDER * RANK]
+            )
 
         def outer(product, left, right):
             shape = [P, left.shape[1], left.shape[2], right.shape[2]]
@@ -105,17 +117,27 @@ def tile_fast_tucker_taylor_pa_k_kernel(tc, z, G2_words, G2_scales, out):
         dc = keep.tile([P, SAMPLE_TILES, RANK * RANK], F32)
         abcd = keep.tile([P, SAMPLE_TILES, 2, P], F32)
         hf_scale = keep.tile([P, SAMPLE_TILES, STEPS_PER_HALF], F32)
-        for u in range(2):
-            outer(ab[:, :, u, :], factor(1), factor(0)[:, :, 2 * u : 2 * u + 2])
-        outer(dc[:], factor(3), factor(2))
-        outer(hf_scale[:], factor(6), factor(5))
+
+        def small_products(half):
+            tiles = tiles_of(half)
+
+            def factor(j):
+                return z_cols[:, tiles, j * RANK : (j + 1) * RANK]
+
+            for u in range(2):
+                outer(ab[:, tiles, u, :], factor(1), factor(0)[:, :, 2 * u : 2 * u + 2])
+            outer(dc[:, tiles, :], factor(3), factor(2))
+            for later in (1, 0):
+                first = half * TILES_PER_HALF + 2 * later
+                for u in range(2):
+                    outer(
+                        abcd[:, first : first + 2, u, :],
+                        dc[:, first : first + 2, :],
+                        ab[:, first : first + 2, u, :],
+                    )
+            outer(hf_scale[:, tiles, :], factor(6), factor(5))
 
         low = keep.tile([P, SAMPLE_TILES, LOW], F32)
-
-        def make_abcd(half):
-            tiles = slice(half * TILES_PER_HALF, (half + 1) * TILES_PER_HALF)
-            for u in range(2):
-                outer(abcd[:, tiles, u, :], dc[:, tiles, :], ab[:, tiles, u, :])
 
         def make_low(tile_no, e, on_scalar):
             by_e = low[:, tile_no, :].rearrange("p (eh u el x) -> p eh u el x", eh=2, u=2, el=2)
@@ -133,14 +155,24 @@ def tile_fast_tucker_taylor_pa_k_kernel(tc, z, G2_words, G2_scales, out):
         x_turned = {}
         y_turned = {}
 
+        def product(step, i, on_scalar):
+            half, hf = divmod(step, STEPS_PER_HALF)
+            tile_no = half * TILES_PER_HALF + i
+            piece = piece_pool.tile([P, LOW], BF16, name="piece%d" % i)
+            times_column(
+                on_scalar, piece[:], low[:, tile_no, :], hf_scale[:, tile_no, hf : hf + 1]
+            )
+            pieces[step, i] = piece[:]
+
         def gpsimd_product(step):
             half, hf = divmod(step, STEPS_PER_HALF)
             tile_no = half * TILES_PER_HALF + BY_GPSIMD
-            if step < REUSE:
-                first = keep.tile([P, LOW], BF16, name="first%d" % step)
-                piece = first[:]
+            pair, j = divmod(step, PAIR)
+            if step < GPSIMD_STARTS + PAIR:
+                piece = pieces[PAIR - 1 - j, BY_GPSIMD]
             else:
-                piece = grouped[step - REUSE][:, 0:LOW]
+                read_last = (pair - 1) * PAIR + PAIR - 1 - QUANTISE_LAG
+                piece = grouped[read_last][:, j * LOW : (j + 1) * LOW]
             nc.gpsimd.tensor_scalar(
                 out=piece[:, 0:GPSIMD_COLUMNS],
                 in0=low[:, tile_no, 0:GPSIMD_COLUMNS],
@@ -160,15 +192,6 @@ def tile_fast_tucker_taylor_pa_k_kernel(tc, z, G2_words, G2_scales, out):
                 low[:, tile_no, GPSIMD_COLUMNS:],
                 hf_scale[:, tile_no, hf : hf + 1],
             )
-
-        def product(step, i):
-            half, hf = divmod(step, STEPS_PER_HALF)
-            tile_no = half * TILES_PER_HALF + i
-            piece = piece_pool.tile([P, LOW], BF16, name="piece%d" % i)
-            times_column(
-                i == BY_SCALAR, piece[:], low[:, tile_no, :], hf_scale[:, tile_no, hf : hf + 1]
-            )
-            pieces[step, i] = piece[:]
 
         def grouped_tile(step):
             if step not in grouped:
@@ -232,9 +255,15 @@ def tile_fast_tucker_taylor_pa_k_kernel(tc, z, G2_words, G2_scales, out):
         def quantise(step):
             words = code_pool.tile([P, 2 * HALF], U32, align_bytes=64)
             scales = code_pool.tile([P, 2 * HALF], U8, align_bytes=64)
-            nc.vector.quantize_mx(
-                out=words[:].bitcast(FP8X4), scales=scales[:], in_=grouped[step][:]
-            )
+            parts = 2 if step == STEPS - 1 else 1
+            width = 2 * HALF // parts
+            for part in range(parts):
+                columns = slice(part * width, (part + 1) * width)
+                nc.vector.quantize_mx(
+                    out=words[:, columns].bitcast(FP8X4),
+                    scales=scales[:, columns],
+                    in_=grouped[step][:, part * width * RANK : (part + 1) * width * RANK],
+                )
             codes[step] = (words, scales)
 
         def multiply(step, eh):
@@ -267,38 +296,49 @@ def tile_fast_tucker_taylor_pa_k_kernel(tc, z, G2_words, G2_scales, out):
                     out=out[m * P : (m + 1) * P, half * HALF : (half + 1) * HALF], in_=result[:]
                 )
 
-        make_abcd(0)
-        for i in (BY_VECTOR, BY_GPSIMD, BY_SCALAR, ROAD_B):
+        turn_z(0)
+        keep_z(0)
+        turn_z(1)
+        small_products(0)
+        for i in (BY_VECTOR, BY_GPSIMD, ROAD_B, BY_SCALAR):
             for e in range(RANK):
                 make_low(i, e, on_scalar=i in (BY_SCALAR, ROAD_B))
-        gpsimd_product(0)
+        keep_z(1)
         turn_scales(0)
         turn_low(0)
-        for tick in range(STEPS + 4):
-            if tick == STEPS_PER_HALF + 4:
-                store(0)
-            if tick == PREPARE_TICK:
-                make_abcd(1)
-            if PREPARE_TICK < tick <= PREPARE_TICK + TILES_PER_HALF:
-                tile_no = TILES_PER_HALF + tick - PREPARE_TICK - 1
-                for e in range(RANK):
-                    make_low(tile_no, e, on_scalar=e >= RANK // 2)
-            if 3 <= tick <= STEPS + 2:
-                quantise(tick - 3)
-            if tick < STEPS:
-                product(tick, BY_VECTOR)
-                product(tick, BY_SCALAR)
-                finish_gpsimd_product(tick)
-            if tick + 1 < STEPS:
-                gpsimd_product(tick + 1)
-            if tick % Y_STEPS == 1 and tick + Y_STEPS < STEPS:
-                turn_scales(tick // Y_STEPS + 1)
-            if 1 <= tick <= STEPS:
-                product_b(tick - 1)
-                turn(tick - 1)
-            if tick == PREPARE_TICK + TILES_PER_HALF + 1:
+        for pair in range((STEPS + MULTIPLY_LAG + PAIR - 1) // PAIR):
+            if pair == PREPARE_PAIR:
+                small_products(1)
+            for tick in range(pair * PAIR, (pair + 1) * PAIR):
+                i = tick - (PREPARE_PAIR + 1) * PAIR
+                if 0 <= i < TILES_PER_HALF:
+                    for e in range(RANK):
+                        make_low(TILES_PER_HALF + i, e, on_scalar=e >= RANK // 2)
+                if tick == STEPS_PER_HALF + MULTIPLY_LAG:
+                    store(0)
+                if QUANTISE_LAG <= tick < STEPS + QUANTISE_LAG:
+                    quantise(tick - QUANTISE_LAG)
+                if tick < STEPS:
+                    product(tick, BY_VECTOR, on_scalar=tick == STEPS - 1)
+                    if tick < GPSIMD_STARTS:
+                        product(tick, BY_GPSIMD, on_scalar=False)
+                    product(tick, BY_SCALAR, on_scalar=tick > 0)
+                    if tick >= GPSIMD_STARTS:
+                        finish_gpsimd_product(tick)
+                turned = tick - PAIR
+                if 0 <= turned < STEPS:
+                    if turned % Y_STEPS == 0 and turned + Y_STEPS < STEPS:
+                        turn_scales(turned // Y_STEPS + 1)
+                    turn(turned)
+                if MULTIPLY_LAG <= tick < STEPS + MULTIPLY_LAG:
+                    for eh in range(2):
+                        multiply(tick - MULTIPLY_LAG, eh)
+            for step in range((pair + 1) * PAIR, (pair + 2) * PAIR):
+                if GPSIMD_STARTS <= step < STEPS:
+                    gpsimd_product(step)
+            for step in range((pair - 1) * PAIR, pair * PAIR):
+                if 0 <= step < STEPS:
+                    product_b(step)
+            if pair == PREPARE_PAIR + 1 + TILES_PER_HALF // PAIR:
                 turn_low(1)
-            if 4 <= tick:
-                for eh in range(2):
-                    multiply(tick - 4, eh)
         store(1)

@@ -92,9 +92,11 @@ def tile_fast_tucker_taylor_pa_k_kernel(tc, z, G2_words, G2_scales, out):
             return slice(half * TILES_PER_HALF, (half + 1) * TILES_PER_HALF)
 
         def keep_z(half):
-            nc.vector.tensor_copy(
-                out=z_cols[:, tiles_of(half), :], in_=z_turned[half][:, :, 0 : ORDER * RANK]
-            )
+            together = z_turned[half][:, :, 0 : ORDER * RANK]
+            if half == 0:
+                nc.vector.tensor_copy(out=z_cols[:, tiles_of(half), :], in_=together)
+            else:
+                nc.scalar.copy(out=z_cols[:, tiles_of(half), :], in_=together)
 
         def outer(product, left, right):
             shape = [P, left.shape[1], left.shape[2], right.shape[2]]
@@ -299,11 +301,11 @@ def tile_fast_tucker_taylor_pa_k_kernel(tc, z, G2_words, G2_scales, out):
         turn_z(0)
         keep_z(0)
         turn_z(1)
-        small_products(0)
-        for i in (BY_VECTOR, BY_GPSIMD, ROAD_B, BY_SCALAR):
-            for e in range(RANK):
-                make_low(i, e, on_scalar=i in (BY_SCALAR, ROAD_B))
         keep_z(1)
+        small_products(0)
+        for i in (ROAD_B, BY_SCALAR, BY_VECTOR, BY_GPSIMD):
+            for e in range(RANK):
+                make_low(i, e, on_scalar=i == BY_SCALAR or (i == ROAD_B and e < RANK // 2))
         turn_scales(0)
         turn_low(0)
         for pair in range((STEPS + MULTIPLY_LAG + PAIR - 1) // PAIR):
@@ -313,17 +315,17 @@ def tile_fast_tucker_taylor_pa_k_kernel(tc, z, G2_words, G2_scales, out):
                 i = tick - (PREPARE_PAIR + 1) * PAIR
                 if 0 <= i < TILES_PER_HALF:
                     for e in range(RANK):
-                        make_low(TILES_PER_HALF + i, e, on_scalar=e >= RANK // 2)
+                        make_low(TILES_PER_HALF + i, e, on_scalar=e == RANK - 1)
                 if tick == STEPS_PER_HALF + MULTIPLY_LAG:
                     store(0)
                 if QUANTISE_LAG <= tick < STEPS + QUANTISE_LAG:
                     quantise(tick - QUANTISE_LAG)
                 if tick < STEPS:
-                    product(tick, BY_VECTOR, on_scalar=tick == STEPS - 1)
+                    product(tick, BY_VECTOR, on_scalar=False)
+                    product(tick, BY_SCALAR, on_scalar=True)
                     if tick < GPSIMD_STARTS:
                         product(tick, BY_GPSIMD, on_scalar=False)
-                    product(tick, BY_SCALAR, on_scalar=tick > 0)
-                    if tick >= GPSIMD_STARTS:
+                    else:
                         finish_gpsimd_product(tick)
                 turned = tick - PAIR
                 if 0 <= turned < STEPS:

@@ -32,7 +32,7 @@ GPSIMD_COLUMNS = 864
 GPSIMD_STARTS = 2 * PAIR
 Y_STEPS = 4
 QUANTISE_LAG = 2 * PAIR
-MULTIPLY_LAG = QUANTISE_LAG + 1
+MULTIPLY_LAG = QUANTISE_LAG + PAIR
 PREPARE_PAIR = 3
 
 FLOPS = 2 * ROWS * RANK**ORDER * SAMPLES
@@ -45,7 +45,7 @@ def tile_fast_tucker_taylor_pa_k_kernel(tc, z, G2_words, G2_scales, out):
         keep = ctx.enter_context(tc.tile_pool(name="keep", bufs=1))
         piece_pool = ctx.enter_context(tc.tile_pool(name="pieces", bufs=2 * PAIR))
         grouped_pool = ctx.enter_context(tc.tile_pool(name="grouped", bufs=4 * PAIR))
-        code_pool = ctx.enter_context(tc.tile_pool(name="codes", bufs=3))
+        code_pool = ctx.enter_context(tc.tile_pool(name="codes", bufs=2 * PAIR))
         result_pool = ctx.enter_context(tc.tile_pool(name="results", bufs=2))
         sums_pool = ctx.enter_context(tc.psum_pool(name="sums", bufs=1))
         y_pool = ctx.enter_context(tc.psum_pool(name="y", bufs=2))
@@ -173,7 +173,7 @@ def tile_fast_tucker_taylor_pa_k_kernel(tc, z, G2_words, G2_scales, out):
             if step < GPSIMD_STARTS + PAIR:
                 piece = pieces[PAIR - 1 - j, BY_GPSIMD]
             else:
-                read_last = (pair - 1) * PAIR + PAIR - 1 - QUANTISE_LAG
+                read_last = (pair - 1) * PAIR - QUANTISE_LAG
                 piece = grouped[read_last][:, j * LOW : (j + 1) * LOW]
             nc.gpsimd.tensor_scalar(
                 out=piece[:, 0:GPSIMD_COLUMNS],
@@ -288,15 +288,22 @@ def tile_fast_tucker_taylor_pa_k_kernel(tc, z, G2_words, G2_scales, out):
                 )
 
         def store(half):
-            for m in range(ROWS // P):
-                result = result_pool.tile([P, HALF], F32)
-                if m == 0:
-                    nc.vector.tensor_copy(out=result[:], in_=sums[m][:])
-                else:
-                    nc.scalar.copy(out=result[:], in_=sums[m][:])
-                nc.sync.dma_start(
-                    out=out[m * P : (m + 1) * P, half * HALF : (half + 1) * HALF], in_=result[:]
-                )
+            parts = 1 + half
+            width = HALF // parts
+            results = {}
+            for part in range(parts):
+                columns = slice(part * width, (part + 1) * width)
+                samples = slice(half * HALF + part * width, half * HALF + (part + 1) * width)
+                for m in range(ROWS // P):
+                    if part == 0:
+                        results[m] = result_pool.tile([P, HALF], F32, name="result%d" % m)
+                    if m == 0:
+                        nc.vector.tensor_copy(out=results[m][:, columns], in_=sums[m][:, columns])
+                    else:
+                        nc.scalar.copy(out=results[m][:, columns], in_=sums[m][:, columns])
+                    nc.sync.dma_start(
+                        out=out[m * P : (m + 1) * P, samples], in_=results[m][:, columns]
+                    )
 
         turn_z(0)
         keep_z(0)
@@ -318,8 +325,6 @@ def tile_fast_tucker_taylor_pa_k_kernel(tc, z, G2_words, G2_scales, out):
                         make_low(TILES_PER_HALF + i, e, on_scalar=e == RANK - 1)
                 if tick == STEPS_PER_HALF + MULTIPLY_LAG:
                     store(0)
-                if QUANTISE_LAG <= tick < STEPS + QUANTISE_LAG:
-                    quantise(tick - QUANTISE_LAG)
                 if tick < STEPS:
                     product(tick, BY_VECTOR, on_scalar=False)
                     product(tick, BY_SCALAR, on_scalar=True)
@@ -335,6 +340,9 @@ def tile_fast_tucker_taylor_pa_k_kernel(tc, z, G2_words, G2_scales, out):
                 if MULTIPLY_LAG <= tick < STEPS + MULTIPLY_LAG:
                     for eh in range(2):
                         multiply(tick - MULTIPLY_LAG, eh)
+            for step in range(pair * PAIR - QUANTISE_LAG, (pair + 1) * PAIR - QUANTISE_LAG):
+                if 0 <= step < STEPS:
+                    quantise(step)
             for step in range((pair + 1) * PAIR, (pair + 2) * PAIR):
                 if GPSIMD_STARTS <= step < STEPS:
                     gpsimd_product(step)

@@ -28,7 +28,7 @@ STEPS = 2 * STEPS_PER_HALF
 BY_GPSIMD, BY_VECTOR, BY_SCALAR, ROAD_B = range(4)
 TURNED_TILES = 3
 PAIR = 2
-GPSIMD_COLUMNS = 864
+GPSIMD_COLUMNS = (LOW, LOW * 3 // 4)
 GPSIMD_STARTS = 2 * PAIR
 Y_STEPS = 4
 QUANTISE_LAG = 2 * PAIR
@@ -170,14 +170,15 @@ def tile_fast_tucker_taylor_pa_k_kernel(tc, z, G2_words, G2_scales, out):
             half, hf = divmod(step, STEPS_PER_HALF)
             tile_no = half * TILES_PER_HALF + BY_GPSIMD
             pair, j = divmod(step, PAIR)
+            share = GPSIMD_COLUMNS[j]
             if step < GPSIMD_STARTS + PAIR:
                 piece = pieces[PAIR - 1 - j, BY_GPSIMD]
             else:
                 read_last = (pair - 1) * PAIR - QUANTISE_LAG
                 piece = grouped[read_last][:, j * LOW : (j + 1) * LOW]
             nc.gpsimd.tensor_scalar(
-                out=piece[:, 0:GPSIMD_COLUMNS],
-                in0=low[:, tile_no, 0:GPSIMD_COLUMNS],
+                out=piece[:, 0:share],
+                in0=low[:, tile_no, 0:share],
                 scalar1=hf_scale[:, tile_no, hf : hf + 1],
                 scalar2=0.0,
                 op0=MULT,
@@ -188,10 +189,11 @@ def tile_fast_tucker_taylor_pa_k_kernel(tc, z, G2_words, G2_scales, out):
         def finish_gpsimd_product(step):
             half, hf = divmod(step, STEPS_PER_HALF)
             tile_no = half * TILES_PER_HALF + BY_GPSIMD
+            share = GPSIMD_COLUMNS[step % PAIR]
             times_column(
                 True,
-                pieces[step, BY_GPSIMD][:, GPSIMD_COLUMNS:],
-                low[:, tile_no, GPSIMD_COLUMNS:],
+                pieces[step, BY_GPSIMD][:, share:],
+                low[:, tile_no, share:],
                 hf_scale[:, tile_no, hf : hf + 1],
             )
 
@@ -330,7 +332,7 @@ def tile_fast_tucker_taylor_pa_k_kernel(tc, z, G2_words, G2_scales, out):
                     product(tick, BY_SCALAR, on_scalar=True)
                     if tick < GPSIMD_STARTS:
                         product(tick, BY_GPSIMD, on_scalar=False)
-                    else:
+                    elif GPSIMD_COLUMNS[tick % PAIR] < LOW:
                         finish_gpsimd_product(tick)
                 turned = tick - PAIR
                 if 0 <= turned < STEPS:

from contextlib import ExitStack

import concourse.mybir as mybir
from concourse.masks import make_identity

F32 = mybir.dt.float32
BF16 = mybir.dt.bfloat16
I32 = mybir.dt.int32
U32 = mybir.dt.uint32
U8 = mybir.dt.uint8
FP8X4 = mybir.dt.float8_e4m3fn_x4
MULT = mybir.AluOpType.mult
ADD = mybir.AluOpType.add
COPY = mybir.ActivationFunctionType.Copy

P = 128
RANK = 4
ORDER = 7
SAMPLES = 1024
ROWS = 256
PASSES = 32
SAMPLE_TILES = SAMPLES // P
HALF = 512
TILES_PER_HALF = HALF // P
LOW = RANK**5
STEPS_PER_HALF = RANK * RANK
STEPS = 2 * STEPS_PER_HALF
BY_GPSIMD, BY_VECTOR, BY_SCALAR, ROAD_B = range(4)
TURNED_TILES = 3
PAIR = 2
GPSIMD_COLUMNS = (LOW, LOW * 3 // 4)
GPSIMD_STARTS = 2 * PAIR
Y_STEPS = 4
QUANTISE_LAG = 2 * PAIR
MULTIPLY_LAG = QUANTISE_LAG + PAIR
PREPARE_PAIR = 3

FLOPS = 2 * ROWS * RANK**ORDER * SAMPLES


def tile_fast_tucker_taylor_pa_k_kernel(tc, z, G2_words, G2_scales, out):
    nc = tc.nc
    with ExitStack() as ctx:
        ctx.enter_context(tc.manual_schedule())
        keep = ctx.enter_context(tc.tile_pool(name="keep", bufs=1))
        piece_pool = ctx.enter_context(tc.tile_pool(name="pieces", bufs=2 * PAIR))
        grouped_pool = ctx.enter_context(tc.tile_pool(name="grouped", bufs=4 * PAIR))
        code_pool = ctx.enter_context(tc.tile_pool(name="codes", bufs=2 * PAIR))
        result_pool = ctx.enter_context(tc.tile_pool(name="results", bufs=2))
        sums_pool = ctx.enter_context(tc.psum_pool(name="sums", bufs=1))
        y_pool = ctx.enter_context(tc.psum_pool(name="y", bufs=2))
        bank_pool = ctx.enter_context(tc.psum_pool(name="banks", bufs=4))

        ident_bf16 = keep.tile([P, P], BF16)
        make_identity(nc, ident_bf16[:])
        z_rows = keep.tile([P, SAMPLES], BF16)
        nc.sync.dma_start(out=z_rows[0 : ORDER * RANK, :], in_=z.rearrange("j r n -> (j r) n"))
        nc.sync.dma_start(out=z_rows[ORDER * RANK : 32, :], in_=z[0])
        nc.vector.memset(z_rows[32:64, :].bitcast(I32), 0)
        nc.vector.memset(z_rows[64:P, :].bitcast(I32), 0)

        g2_scales = keep.tile([P, PASSES, ROWS], U8, align_bytes=64)
        nc.vector.memset(g2_scales[:].bitcast(I32), 0)
        for r in range(4):
            nc.sync.dma_start(
                out=g2_scales[r:P:32, :, :].bitcast(I32),
                in_=G2_scales.rearrange("g (quad r) n -> r quad g n", r=4)[r].bitcast(I32),
            )
        g2_words = keep.tile([P, PASSES, ROWS], U32, align_bytes=64)
        for g in range(0, PASSES, 4):
            nc.sync.dma_start(
                out=g2_words[:, g : g + 4, :].bitcast(I32),
                in_=G2_words[g : g + 4].rearrange("g p n t -> p g (n t)").bitcast(I32),
            )

        ident_f32 = keep.tile([P, P], F32)
        make_identity(nc, ident_f32[:])

        z_cols = keep.tile([P, SAMPLE_TILES, ORDER * RANK], F32)
        z_turned = {}

        def turn_z(half):
            z_bank = bank_pool.tile([P, TILES_PER_HALF, P], BF16, tag="bank")
            for i in range(TILES_PER_HALF):
                tile_no = half * TILES_PER_HALF + i
                nc.tensor.transpose(
                    z_bank[:, i, :], z_rows[:, tile_no * P : (tile_no + 1) * P], ident_bf16[:]
                )
            z_turned[half] = z_bank

        def tiles_of(half):
            return slice(half * TILES_PER_HALF, (half + 1) * TILES_PER_HALF)

        def keep_z(half):
            together = z_turned[half][:, :, 0 : ORDER * RANK]
            if half == 0:
                nc.vector.tensor_copy(out=z_cols[:, tiles_of(half), :], in_=together)
            else:
                nc.scalar.copy(out=z_cols[:, tiles_of(half), :], in_=together)

        def outer(product, left, right):
            shape = [P, left.shape[1], left.shape[2], right.shape[2]]
            nc.vector.tensor_tensor(
                out=product.rearrange("p j (x y) -> p j x y", y=right.shape[2]),
                in0=left.unsqueeze(3).to_broadcast(shape),
                in1=right.unsqueeze(2).to_broadcast(shape),
                op=MULT,
            )

        def times_column(on_scalar, product, values, column):
            if on_scalar:
                nc.scalar.activation(out=product, in_=values, func=COPY, scale=column)
            else:
                nc.vector.tensor_scalar(
                    out=product, in0=values, scalar1=column, scalar2=None, op0=MULT
                )

        ab = keep.tile([P, SAMPLE_TILES, 2, 2 * RANK], F32)
        dc = keep.tile([P, SAMPLE_TILES, RANK * RANK], F32)
        abcd = keep.tile([P, SAMPLE_TILES, 2, P], F32)
        hf_scale = keep.tile([P, SAMPLE_TILES, STEPS_PER_HALF], F32)

        def small_products(half):
            tiles = tiles_of(half)

            def factor(j):
                return z_cols[:, tiles, j * RANK : (j + 1) * RANK]

            for u in range(2):
                outer(ab[:, tiles, u, :], factor(1), factor(0)[:, :, 2 * u : 2 * u + 2])
            outer(dc[:, tiles, :], factor(3), factor(2))
            for later in (1, 0):
                first = half * TILES_PER_HALF + 2 * later
                for u in range(2):
                    outer(
                        abcd[:, first : first + 2, u, :],
                        dc[:, first : first + 2, :],
                        ab[:, first : first + 2, u, :],
                    )
            outer(hf_scale[:, tiles, :], factor(6), factor(5))

        low = keep.tile([P, SAMPLE_TILES, LOW], F32)

        def make_low(tile_no, e, on_scalar):
            by_e = low[:, tile_no, :].rearrange("p (eh u el x) -> p eh u el x", eh=2, u=2, el=2)
            times_column(
                on_scalar,
                by_e[:, e // 2, :, e % 2, :],
                abcd[:, tile_no],
                z_cols[:, tile_no, 4 * RANK + e : 4 * RANK + e + 1],
            )

        pieces = {}
        grouped = {}
        codes = {}
        sums = {}
        x_turned = {}
        y_turned = {}

        def product(step, i, on_scalar):
            half, hf = divmod(step, STEPS_PER_HALF)
            tile_no = half * TILES_PER_HALF + i
            piece = piece_pool.tile([P, LOW], BF16, name="piece%d" % i)
            times_column(
                on_scalar, piece[:], low[:, tile_no, :], hf_scale[:, tile_no, hf : hf + 1]
            )
            pieces[step, i] = piece[:]

        def gpsimd_product(step):
            half, hf = divmod(step, STEPS_PER_HALF)
            tile_no = half * TILES_PER_HALF + BY_GPSIMD
            pair, j = divmod(step, PAIR)
            share = GPSIMD_COLUMNS[j]
            if step < GPSIMD_STARTS + PAIR:
                piece = pieces[PAIR - 1 - j, BY_GPSIMD]
            else:
                read_last = (pair - 1) * PAIR - QUANTISE_LAG
                piece = grouped[read_last][:, j * LOW : (j + 1) * LOW]
            nc.gpsimd.tensor_scalar(
                out=piece[:, 0:share],
                in0=low[:, tile_no, 0:share],
                scalar1=hf_scale[:, tile_no, hf : hf + 1],
                scalar2=0.0,
                op0=MULT,
                op1=ADD,
            )
            pieces[step, BY_GPSIMD] = piece

        def finish_gpsimd_product(step):
            half, hf = divmod(step, STEPS_PER_HALF)
            tile_no = half * TILES_PER_HALF + BY_GPSIMD
            share = GPSIMD_COLUMNS[step % PAIR]
            times_column(
                True,
                pieces[step, BY_GPSIMD][:, share:],
                low[:, tile_no, share:],
                hf_scale[:, tile_no, hf : hf + 1],
            )

        def grouped_tile(step):
            if step not in grouped:
                together = grouped_pool.tile([P, 2 * HALF * RANK], BF16, align_bytes=64)
                grouped[step] = together
            return grouped[step]

        def turn(step):
            pairs = grouped_tile(step)[:].bitcast(F32).rearrange(
                "p (eh i n u) -> p eh i n u", eh=2, i=TILES_PER_HALF, u=2
            )
            for i in range(TURNED_TILES):
                bank = bank_pool.tile([P, 2, 2, P], F32, tag="bank")
                piece_pairs = pieces[step, i].bitcast(F32)
                for eh in range(2):
                    for u in range(2):
                        first = (2 * eh + u) * P
                        nc.tensor.transpose(
                            bank[:, eh, u, :], piece_pairs[:, first : first + P], ident_f32[:]
                        )
                nc.scalar.copy(out=pairs[:, :, i], in_=bank[:].rearrange("p e u n -> p e n u"))

        def turn_low(half):
            tile_no = half * TILES_PER_HALF + ROAD_B
            x = keep.tile([P, 2, P, RANK], F32, name="x%d" % half)
            for eh in range(2):
                bank = bank_pool.tile([P, RANK, P], F32, tag="bank")
                for a in range(RANK):
                    first = (2 * eh + a // 2) * 2 * P + a % 2
                    nc.tensor.transpose(
                        bank[:, a, :], low[:, tile_no, first : first + 2 * P - 1 : 2], ident_f32[:]
                    )
                nc.scalar.copy(out=x[:, eh], in_=bank[:].rearrange("p a n -> p n a"))
            x_turned[half] = x

        def turn_scales(group):
            y = y_pool.tile([P, Y_STEPS, P], F32)
            for j in range(Y_STEPS):
                half, hf = divmod(Y_STEPS * group + j, STEPS_PER_HALF)
                tile_no = half * TILES_PER_HALF + ROAD_B
                nc.tensor.transpose(
                    y[:, j, :],
                    hf_scale[:, tile_no, hf : hf + 1].to_broadcast([P, P]),
                    ident_f32[:],
                )
            y_turned[group] = y

        def product_b(step):
            shape = [P, 2, P, RANK]
            columns = grouped_tile(step)[:].rearrange(
                "p (eh i n a) -> p eh i n a", eh=2, i=TILES_PER_HALF, a=RANK
            )[:, :, ROAD_B]
            y = y_turned[step // Y_STEPS][:, step % Y_STEPS, :]
            nc.vector.tensor_tensor(
                out=columns,
                in0=x_turned[step // STEPS_PER_HALF][:],
                in1=y.unsqueeze(1).unsqueeze(3).to_broadcast(shape),
                op=MULT,
            )

        def quantise(step):
            words = code_pool.tile([P, 2 * HALF], U32, align_bytes=64)
            scales = code_pool.tile([P, 2 * HALF], U8, align_bytes=64)
            parts = 2 if step == STEPS - 1 else 1
            width = 2 * HALF // parts
            for part in range(parts):
                columns = slice(part * width, (part + 1) * width)
                nc.vector.quantize_mx(
                    out=words[:, columns].bitcast(FP8X4),
                    scales=scales[:, columns],
                    in_=grouped[step][:, part * width * RANK : (part + 1) * width * RANK],
                )
            codes[step] = (words, scales)

        def multiply(step, eh):
            g = 2 * (step % STEPS_PER_HALF) + eh
            words, scales = codes[step]
            if g == 0:
                for m in range(ROWS // P):
                    sums[m] = sums_pool.tile([P, HALF], F32, name="sums%d" % m)
            columns = slice(eh * HALF, (eh + 1) * HALF)
            for m in range(ROWS // P):
                rows = slice(m * P, (m + 1) * P)
                nc.tensor.matmul_mx(
                    out=sums[m][:],
                    lhsT=g2_words[:, g, rows].bitcast(FP8X4),
                    lhsT_scale=g2_scales[:, g, rows],
                    rhs=words[:, columns].bitcast(FP8X4),
                    rhs_scale=scales[:, columns],
                    start=(g == 0),
                    stop=(g == PASSES - 1),
                )

        def store(half):
            parts = 1 + half
            width = HALF // parts
            results = {}
            for part in range(parts):
                columns = slice(part * width, (part + 1) * width)
                samples = slice(half * HALF + part * width, half * HALF + (part + 1) * width)
                for m in range(ROWS // P):
                    if part == 0:
                        results[m] = result_pool.tile([P, HALF], F32, name="result%d" % m)
                    if m == 0:
                        nc.vector.tensor_copy(out=results[m][:, columns], in_=sums[m][:, columns])
                    else:
                        nc.scalar.copy(out=results[m][:, columns], in_=sums[m][:, columns])
                    nc.sync.dma_start(
                        out=out[m * P : (m + 1) * P, samples], in_=results[m][:, columns]
                    )

        turn_z(0)
        keep_z(0)
        turn_z(1)
        keep_z(1)
        small_products(0)
        for i in (ROAD_B, BY_SCALAR, BY_VECTOR, BY_GPSIMD):
            for e in range(RANK):
                make_low(i, e, on_scalar=i == BY_SCALAR or (i == ROAD_B and e < RANK // 2))
        turn_scales(0)
        turn_low(0)
        for pair in range((STEPS + MULTIPLY_LAG + PAIR - 1) // PAIR):
            if pair == PREPARE_PAIR:
                small_products(1)
            for tick in range(pair * PAIR, (pair + 1) * PAIR):
                i = tick - (PREPARE_PAIR + 1) * PAIR
                if 0 <= i < TILES_PER_HALF:
                    for e in range(RANK):
                        make_low(TILES_PER_HALF + i, e, on_scalar=e == RANK - 1)
                if tick == STEPS_PER_HALF + MULTIPLY_LAG:
                    store(0)
                if tick < STEPS:
                    product(tick, BY_VECTOR, on_scalar=False)
                    product(tick, BY_SCALAR, on_scalar=True)
                    if tick < GPSIMD_STARTS:
                        product(tick, BY_GPSIMD, on_scalar=False)
                    elif GPSIMD_COLUMNS[tick % PAIR] < LOW:
                        finish_gpsimd_product(tick)
                turned = tick - PAIR
                if 0 <= turned < STEPS:
                    if turned % Y_STEPS == 0 and turned + Y_STEPS < STEPS:
                        turn_scales(turned // Y_STEPS + 1)
                    turn(turned)
                if MULTIPLY_LAG <= tick < STEPS + MULTIPLY_LAG:
                    for eh in range(2):
                        multiply(tick - MULTIPLY_LAG, eh)
            for step in range(pair * PAIR - QUANTISE_LAG, (pair + 1) * PAIR - QUANTISE_LAG):
                if 0 <= step < STEPS:
                    quantise(step)
            for step in range((pair + 1) * PAIR, (pair + 2) * PAIR):
                if GPSIMD_STARTS <= step < STEPS:
                    gpsimd_product(step)
            for step in range((pair - 1) * PAIR, pair * PAIR):
                if 0 <= step < STEPS:
                    product_b(step)
            if pair == PREPARE_PAIR + 1 + TILES_PER_HALF // PAIR:
                turn_low(1)
        store(1)
